import numpy as np
import ml_dtypes


def mxq(x, axis, fmt="e4m3"):
    dtype, down = {"e4m3": (ml_dtypes.float8_e4m3fn, 7), "e5m2": (ml_dtypes.float8_e5m2, 14)}[fmt]
    v = np.moveaxis(np.asarray(x, np.float32).astype(ml_dtypes.bfloat16).astype(np.float64), axis, -1)
    blocks = v.reshape(v.shape[:-1] + (-1, 32))
    amax = np.abs(blocks).max(-1, keepdims=True)
    byte = np.maximum(np.where(amax > 0, np.frexp(amax)[1] - 1 + 127, 0) - down, 1)
    scale = np.exp2(byte - 127.0)
    codes = (blocks / scale).astype(np.float32).astype(dtype).astype(np.float64)
    return np.moveaxis((codes * scale).reshape(v.shape), -1, axis)


WIDE = False


def mx_kscale(k):
    if not WIDE:
        return np.ones(k)
    levels = np.array([10, -10, 5, -5, 0])
    a = np.random.permutation(np.resize(levels, k // 512 * 4)).reshape(k // 512, 4)
    idx = np.arange(k)
    return np.exp2(a[idx // 512, idx % 128 // 32])


BF16 = ml_dtypes.bfloat16


def bf(x):
    return np.asarray(x, np.float32).astype(BF16)


def f64(x):
    return np.asarray(x).astype(np.float64)


B, S, D_MODEL, N_H, D_H, D_CQ, D_CKV, D_HR = 4, 1024, 1024, 4, 128, 512, 512, 128
ROPE_BASE = 10000.0


def rope_cos_sin(seq_len, dim):
    inv_freq = 1.0 / (ROPE_BASE ** (np.arange(0, dim, 2) / dim))
    ang = np.arange(seq_len)[:, None] * inv_freq[None, :]
    return np.cos(ang), np.sin(ang)


def rope(t, cos, sin):
    shp = t.shape
    d2 = shp[-1] // 2
    tr = t.reshape(shp[:-1] + (d2, 2))
    x0, x1 = tr[..., 0], tr[..., 1]
    bshape = (1, shp[1]) + (1,) * (x0.ndim - 3) + (d2,)
    cs, sn = cos.reshape(bshape), sin.reshape(bshape)
    return np.stack([x0 * cs - x1 * sn, x0 * sn + x1 * cs], axis=-1).reshape(shp)


def setup_inputs():
    s, t = mx_kscale(D_MODEL), mx_kscale(D_CQ)
    return {"h": bf(np.random.standard_normal((B, S, D_MODEL)) * s),
            "w_cq": bf(np.random.standard_normal((D_MODEL, D_CQ)) / np.sqrt(D_MODEL) / s[:, None] * t),
            "w_q": bf(np.random.standard_normal((D_CQ, N_H * D_H)) / np.sqrt(D_CQ) / t[:, None]),
            "w_qr": bf(np.random.standard_normal((D_CQ, N_H * D_HR)) / np.sqrt(D_CQ) / t[:, None])}


def reference(h, w_cq, w_q, w_qr):
    cos, sin = rope_cos_sin(S, D_HR)
    c_q = mxq(f64(h), 2, "e4m3") @ mxq(f64(w_cq), 0, "e4m3")
    cq = mxq(c_q, 2, "e4m3")
    q_c = (cq @ mxq(f64(w_q), 0, "e4m3")).reshape(B, S, N_H, D_H).transpose(0, 2, 1, 3)
    q_r = rope((cq @ mxq(f64(w_qr), 0, "e4m3")).reshape(B, S, N_H, D_HR), cos, sin).transpose(0, 2, 1, 3)
    return np.concatenate([q_c, q_r], axis=-1)

@@ -1,0 +1,249 @@
+import math
+from contextlib import ExitStack
+
+import concourse.mybir as mybir
+from concourse.masks import make_identity
+
+F32 = mybir.dt.float32
+BF16 = mybir.dt.bfloat16
+I32 = mybir.dt.int32
+U32 = mybir.dt.uint32
+U8 = mybir.dt.uint8
+FP8X4 = mybir.dt.float8_e4m3fn_x4
+MULT = mybir.AluOpType.mult
+ADD = mybir.AluOpType.add
+SUBTRACT = mybir.AluOpType.subtract
+SIN = mybir.ActivationFunctionType.Sin
+
+P = 128
+PACK = 4
+B, S, D_MODEL, N_H, D_H, D_CQ = 4, 1024, 1024, 4, 128, 512
+PASSES_1 = D_MODEL // (P * PACK)
+TILES = S // P
+PAIRS = D_H // 2
+HALF = 4
+STEP = 2
+ROPE_BASE = 10000.0
+ROUND_MAGIC = 1.5 * 2.0**23
+
+FLOPS = 2 * B * S * (D_MODEL * D_CQ + D_CQ * 2 * N_H * D_H)
+
+
+def build_rope_tables(nc, pool):
+    position_i = pool.tile([P, TILES], I32)
+    nc.gpsimd.iota(position_i[:], pattern=[[1, TILES]], base=0, channel_multiplier=TILES)
+    position = pool.tile([P, TILES], F32)
+    nc.vector.tensor_copy(out=position[:], in_=position_i[:])
+
+    ratio = ROPE_BASE ** (-1.0 / PAIRS)
+    freq = pool.tile([P, PAIRS], F32)
+    nc.vector.memset(freq[:, 0:1], 1.0)
+    for level in range(6):
+        w = 2**level
+        nc.vector.tensor_scalar_mul(out=freq[:, w : 2 * w], in0=freq[:, 0:w], scalar1=ratio**w)
+
+    shape = [P, TILES, PAIRS]
+    turns = pool.tile(shape, F32)
+    nc.vector.scalar_tensor_tensor(
+        out=turns[:],
+        in0=freq[:].unsqueeze(1).to_broadcast(shape),
+        scalar=1.0 / (2.0 * math.pi),
+        in1=position[:].unsqueeze(2).to_broadcast(shape),
+        op0=MULT,
+        op1=MULT,
+    )
+    quarter = pool.tile(shape, F32)
+    nc.vector.tensor_scalar_add(out=quarter[:], in0=turns[:], scalar1=0.25)
+
+    fractions = []
+    for name, angle in (("sin", turns), ("cos", quarter)):
+        whole = pool.tile(shape, F32, name="whole_" + name)
+        nc.vector.tensor_scalar(
+            out=whole[:], in0=angle[:], scalar1=ROUND_MAGIC, scalar2=ROUND_MAGIC, op0=ADD, op1=SUBTRACT
+        )
+        fraction = pool.tile(shape, F32, name="fraction_" + name)
+        nc.vector.tensor_sub(out=fraction[:], in0=angle[:], in1=whole[:])
+        fractions.append(fraction)
+    sin_fraction, cos_fraction = fractions
+
+    sin2 = pool.tile([P, TILES, 2, PAIRS], F32)
+    nc.scalar.activation(out=sin2[:, :, 0, :], in_=sin_fraction[:], func=SIN, scale=-2.0 * math.pi)
+    nc.scalar.activation(out=sin2[:, :, 1, :], in_=sin_fraction[:], func=SIN, scale=2.0 * math.pi)
+    cos2 = pool.tile([P, TILES, PAIRS, 2], F32)
+    nc.scalar.activation(
+        out=cos2[:],
+        in_=cos_fraction[:].unsqueeze(3).to_broadcast([P, TILES, PAIRS, 2]),
+        func=SIN,
+        scale=2.0 * math.pi,
+    )
+    return cos2, sin2
+
+
+def quantise_weight(nc, pool, name, raw, codes, scales):
+    cols = raw.shape[2]
+    grouped = pool.tile([P, cols, PACK], BF16, name="grouped_" + name, align_bytes=64)
+    nc.vector.tensor_copy(out=grouped[:], in_=raw.rearrange("p t c -> p c t"))
+    nc.vector.quantize_mx(
+        out=codes.bitcast(FP8X4), scales=scales, in_=grouped[:].rearrange("p c t -> p (c t)")
+    )
+
+
+def tile_mla_pa_t_kernel(tc, h, w_cq, w_q, w_qr, out):
+    nc = tc.nc
+    with ExitStack() as ctx:
+        consts = ctx.enter_context(tc.tile_pool(name="consts", bufs=1))
+        x_pool = ctx.enter_context(tc.tile_pool(name="x", bufs=B * TILES // HALF))
+        work = ctx.enter_context(tc.tile_pool(name="work", bufs=3))
+        out_pool = ctx.enter_context(tc.tile_pool(name="outs", bufs=3))
+        psum = ctx.enter_context(tc.psum_pool(name="psum", bufs=2))
+
+        halves = [(b, half) for b in range(B) for half in range(TILES // HALF)]
+        x_tiles = {}
+        for b, half in halves:
+            x_tiles[(b, half)] = x_pool.tile([P, HALF, D_MODEL], BF16, name="x")
+
+        def load_h(b, half, first, count):
+            rows = h[b].rearrange("(p t) k -> p t k", t=TILES)
+            nc.sync.dma_start(
+                out=x_tiles[(b, half)][:, first : first + count, :],
+                in_=rows[:, half * HALF + first : half * HALF + first + count, :],
+            )
+
+        wc_raw = consts.tile([P, PASSES_1, PACK, D_CQ], BF16)
+        w2_raw = consts.tile([P, 2, PACK, N_H * D_H], BF16)
+        load_h(0, 0, 0, STEP)
+        nc.sync.dma_start(
+            out=wc_raw[:].rearrange("p g (u e) c -> p (g u) (e c)", u=2),
+            in_=w_cq.rearrange("(a q e) c -> q a (e c)", a=2 * PASSES_1, e=2),
+        )
+        load_h(0, 0, STEP, STEP)
+        nc.sync.dma_start(out=w2_raw[:, 0], in_=w_q.rearrange("(t p) n -> p t n", p=P))
+        nc.sync.dma_start(out=w2_raw[:, 1], in_=w_qr.rearrange("(t p) n -> p t n", p=P))
+        for b, half in halves[1:]:
+            load_h(b, half, 0, HALF)
+
+        identity = consts.tile([P, P], F32)
+        make_identity(nc, identity[:])
+        cos2, sin2 = build_rope_tables(nc, consts)
+
+        wc_codes = consts.tile([P, PASSES_1, D_CQ], U32, align_bytes=64)
+        wc_scales = consts.tile([P, PASSES_1, D_CQ], U8, align_bytes=64)
+        for g in range(PASSES_1):
+            quantise_weight(nc, consts, "wc%d" % g, wc_raw[:, g], wc_codes[:, g, :], wc_scales[:, g, :])
+        w2_codes = consts.tile([P, 2, N_H * D_H], U32, align_bytes=64)
+        w2_scales = consts.tile([P, 2, N_H * D_H], U8, align_bytes=64)
+        for which in range(2):
+            quantise_weight(
+                nc, consts, "w2%d" % which, w2_raw[:, which], w2_codes[:, which, :], w2_scales[:, which, :]
+            )
+
+        steps = [(b, first) for b in range(B) for first in range(0, TILES, STEP)]
+        h_mx = {}
+        c_mx = {}
+        out_tiles = {}
+
+        def transpose_and_quantise_h(n):
+            b, first = steps[n]
+            x_words = x_tiles[(b, first // HALF)][:].rearrange("p t k -> p (t k)").bitcast(F32)
+            grouped = work.tile([P, STEP * PASSES_1 * P * PACK], BF16, name="h_grouped", align_bytes=64)
+            grouped_words = grouped[:].bitcast(F32).rearrange(
+                "p (i g r u) -> p i g r u", i=STEP, g=PASSES_1, u=2
+            )
+            for i in range(STEP):
+                word0 = ((first + i) % HALF) * (D_MODEL // 2)
+                xt = psum.tile([P, 2 * PASSES_1, P], F32, name="xt")
+                for a in range(2 * PASSES_1):
+                    nc.tensor.transpose(xt[:, a, :], x_words[:, word0 + a * P : word0 + (a + 1) * P], identity[:])
+                nc.scalar.copy(out=grouped_words[:, i], in_=xt[:].rearrange("p (g u) r -> p g r u", u=2))
+            codes = work.tile([P, STEP, PASSES_1, P], U32, name="h_codes", align_bytes=64)
+            scales = work.tile([P, STEP, PASSES_1, P], U8, name="h_scales", align_bytes=64)
+            nc.vector.quantize_mx(
+                out=codes[:].rearrange("p i g r -> p (i g r)").bitcast(FP8X4),
+                scales=scales[:].rearrange("p i g r -> p (i g r)"),
+                in_=grouped[:],
+            )
+            h_mx[n] = (codes, scales)
+
+        def compress_and_quantise(n):
+            codes_h, scales_h = h_mx[n]
+            grouped = work.tile([P, STEP, P, PACK], BF16, name="c_grouped", align_bytes=64)
+            for i in range(STEP):
+                cq = psum.tile([P, PACK, P], F32, name="cq")
+                for t in range(PACK):
+                    for g in range(PASSES_1):
+                        nc.tensor.matmul_mx(
+                            out=cq[:, t, :],
+                            lhsT=wc_codes[:, g, t * P : (t + 1) * P].bitcast(FP8X4),
+                            lhsT_scale=wc_scales[:, g, t * P : (t + 1) * P],
+                            rhs=codes_h[:, i, g, :].bitcast(FP8X4),
+                            rhs_scale=scales_h[:, i, g, :],
+                            start=(g == 0),
+                            stop=(g == PASSES_1 - 1),
+                        )
+                nc.scalar.copy(out=grouped[:, i], in_=cq[:].rearrange("p t r -> p r t"))
+            codes = work.tile([P, STEP, P], U32, name="c_codes", align_bytes=64)
+            scales = work.tile([P, STEP, P], U8, name="c_scales", align_bytes=64)
+            nc.vector.quantize_mx(
+                out=codes[:].rearrange("p i r -> p (i r)").bitcast(FP8X4),
+                scales=scales[:].rearrange("p i r -> p (i r)"),
+                in_=grouped[:].rearrange("p i r t -> p (i r t)"),
+            )
+            c_mx[n] = (codes, scales)
+
+        def project_rotate_store(n):
+            b, first = steps[n]
+            codes_c, scales_c = c_mx[n]
+            half = first // HALF
+            if first % HALF == 0:
+                out_tiles[(b, half)] = out_pool.tile([P, N_H, HALF, 2 * D_H], F32, name="q_tile")
+            q_tile = out_tiles[(b, half)]
+            for i in range(STEP):
+                t = first + i
+                products = []
+                for which, name in enumerate(("a_ps", "u_ps")):
+                    product = psum.tile([P, N_H * D_H], F32, name=name)
+                    nc.tensor.matmul_mx(
+                        out=product[:],
+                        lhsT=codes_c[:, i, :].bitcast(FP8X4),
+                        lhsT_scale=scales_c[:, i, :],
+                        rhs=w2_codes[:, which, :].bitcast(FP8X4),
+                        rhs_scale=w2_scales[:, which, :],
+                        start=True,
+                        stop=True,
+                    )
+                    products.append(product)
+                a_ps, u_ps = products
+                nc.scalar.copy(
+                    out=q_tile[:, :, t % HALF, 0:D_H], in_=a_ps[:].rearrange("p (n f) -> p n f", n=N_H)
+                )
+                rotated = q_tile[:, :, t % HALF, D_H : 2 * D_H]
+                nc.vector.tensor_tensor(
+                    out=rotated,
+                    in0=u_ps[:].rearrange("p (n f) -> p n f", n=N_H),
+                    in1=cos2[:, t].rearrange("p i e -> p (i e)").unsqueeze(1).to_broadcast([P, N_H, D_H]),
+                    op=MULT,
+                )
+                u_pairs = u_ps[:].rearrange("p (n i e) -> p n i e", n=N_H, e=2)
+                crossed = work.tile([P, 2, N_H, PAIRS], F32, name="crossed")
+                for e in range(2):
+                    nc.vector.tensor_tensor(
+                        out=crossed[:, e],
+                        in0=u_pairs[:, :, :, 1 - e],
+                        in1=sin2[:, t, e, :].unsqueeze(1).to_broadcast([P, N_H, PAIRS]),
+                        op=MULT,
+                    )
+                rotated_pairs = rotated.rearrange("p n (i e) -> p n i e", e=2)
+                nc.gpsimd.tensor_tensor(
+                    out=rotated_pairs, in0=rotated_pairs, in1=crossed[:].rearrange("p e n i -> p n i e"), op=ADD
+                )
+            if (first + STEP) % HALF == 0:
+                rows = out[b].rearrange("n (p t) f -> p n t f", t=TILES)
+                nc.sync.dma_start(out=rows[:, :, half * HALF : (half + 1) * HALF, :], in_=q_tile[:])
+
+        for n in range(len(steps) + 2):
+            if n < len(steps):
+                transpose_and_quantise_h(n)
+            if 1 <= n <= len(steps):
+                compress_and_quantise(n - 1)
+            if n >= 2:
+                project_rotate_store(n - 2)

@@ -18,6 +18,7 @@ SIN = mybir.ActivationFunctionType.Sin
 P = 128
 PACK = 4
 B, S, D_MODEL, N_H, D_H, D_CQ = 4, 1024, 1024, 4, 128, 512
+D_OUT = N_H * D_H
 PASSES_1 = D_MODEL // (P * PACK)
 TILES = S // P
 PAIRS = D_H // 2
@@ -26,10 +27,10 @@ STEP = 2
 ROPE_BASE = 10000.0
 ROUND_MAGIC = 1.5 * 2.0**23
 
-FLOPS = 2 * B * S * (D_MODEL * D_CQ + D_CQ * 2 * N_H * D_H)
+FLOPS = 2 * B * S * (D_MODEL * D_CQ + D_CQ * 2 * D_OUT)
 
 
-def build_rope_tables(nc, pool):
+def rope_turn_fractions(nc, pool):
     position_i = pool.tile([P, TILES], I32)
     nc.gpsimd.iota(position_i[:], pattern=[[1, TILES]], base=0, channel_multiplier=TILES)
     position = pool.tile([P, TILES], F32)
@@ -64,38 +65,33 @@ def build_rope_tables(nc, pool):
         fraction = pool.tile(shape, F32, name="fraction_" + name)
         nc.vector.tensor_sub(out=fraction[:], in0=angle[:], in1=whole[:])
         fractions.append(fraction)
-    sin_fraction, cos_fraction = fractions
-
-    sin2 = pool.tile([P, TILES, 2, PAIRS], F32)
-    nc.scalar.activation(out=sin2[:, :, 0, :], in_=sin_fraction[:], func=SIN, scale=-2.0 * math.pi)
-    nc.scalar.activation(out=sin2[:, :, 1, :], in_=sin_fraction[:], func=SIN, scale=2.0 * math.pi)
-    cos2 = pool.tile([P, TILES, PAIRS, 2], F32)
-    nc.scalar.activation(
-        out=cos2[:],
-        in_=cos_fraction[:].unsqueeze(3).to_broadcast([P, TILES, PAIRS, 2]),
-        func=SIN,
-        scale=2.0 * math.pi,
-    )
-    return cos2, sin2
+    return fractions
 
 
-def quantise_weight(nc, pool, name, raw, codes, scales):
-    cols = raw.shape[2]
-    grouped = pool.tile([P, cols, PACK], BF16, name="grouped_" + name, align_bytes=64)
-    nc.vector.tensor_copy(out=grouped[:], in_=raw.rearrange("p t c -> p c t"))
-    nc.vector.quantize_mx(
-        out=codes.bitcast(FP8X4), scales=scales, in_=grouped[:].rearrange("p c t -> p (c t)")
+def rope_table(nc, pool, sin_fraction, cos_fraction):
+    table = pool.tile([P, TILES, 3, PAIRS], F32)
+    nc.scalar.activation(out=table[:, :, 0, :], in_=sin_fraction[:], func=SIN, scale=2.0 * math.pi)
+    nc.scalar.activation(out=table[:, :, 2, :], in_=sin_fraction[:], func=SIN, scale=-2.0 * math.pi)
+    nc.scalar.activation(out=table[:, :, 1, :], in_=cos_fraction[:], func=SIN, scale=2.0 * math.pi)
+    return table
+
+
+def regroup(copy, grouped, raw):
+    copy(
+        out=grouped.rearrange("p (c i) t -> p c t i", i=4),
+        in_=raw.rearrange("p t (c i) -> p c t i", i=4),
     )
 
 
 def tile_mla_pa_t_kernel(tc, h, w_cq, w_q, w_qr, out):
     nc = tc.nc
     with ExitStack() as ctx:
+        ctx.enter_context(tc.manual_schedule())
         consts = ctx.enter_context(tc.tile_pool(name="consts", bufs=1))
         x_pool = ctx.enter_context(tc.tile_pool(name="x", bufs=B * TILES // HALF))
         work = ctx.enter_context(tc.tile_pool(name="work", bufs=3))
         out_pool = ctx.enter_context(tc.tile_pool(name="outs", bufs=3))
-        psum = ctx.enter_context(tc.psum_pool(name="psum", bufs=2))
+        psum = ctx.enter_context(tc.psum_pool(name="psum", bufs=STEP))
 
         halves = [(b, half) for b in range(B) for half in range(TILES // HALF)]
         x_tiles = {}
@@ -110,63 +106,84 @@ def tile_mla_pa_t_kernel(tc, h, w_cq, w_q, w_qr, out):
             )
 
         wc_raw = consts.tile([P, PASSES_1, PACK, D_CQ], BF16)
-        w2_raw = consts.tile([P, 2, PACK, N_H * D_H], BF16)
-        load_h(0, 0, 0, STEP)
+        w2_raw = consts.tile([P, 2, PACK, D_OUT], BF16)
         nc.sync.dma_start(
             out=wc_raw[:].rearrange("p g (u e) c -> p (g u) (e c)", u=2),
             in_=w_cq.rearrange("(a q e) c -> q a (e c)", a=2 * PASSES_1, e=2),
         )
+        load_h(0, 0, 0, STEP)
         load_h(0, 0, STEP, STEP)
         nc.sync.dma_start(out=w2_raw[:, 0], in_=w_q.rearrange("(t p) n -> p t n", p=P))
         nc.sync.dma_start(out=w2_raw[:, 1], in_=w_qr.rearrange("(t p) n -> p t n", p=P))
         for b, half in halves[1:]:
             load_h(b, half, 0, HALF)
 
+        sin_fraction, cos_fraction = rope_turn_fractions(nc, consts)
+        table = rope_table(nc, consts, sin_fraction, cos_fraction)
         identity = consts.tile([P, P], F32)
         make_identity(nc, identity[:])
-        cos2, sin2 = build_rope_tables(nc, consts)
 
+        wc_grouped = consts.tile([P, PASSES_1, D_CQ, PACK], BF16, align_bytes=64)
         wc_codes = consts.tile([P, PASSES_1, D_CQ], U32, align_bytes=64)
         wc_scales = consts.tile([P, PASSES_1, D_CQ], U8, align_bytes=64)
         for g in range(PASSES_1):
-            quantise_weight(nc, consts, "wc%d" % g, wc_raw[:, g], wc_codes[:, g, :], wc_scales[:, g, :])
-        w2_codes = consts.tile([P, 2, N_H * D_H], U32, align_bytes=64)
-        w2_scales = consts.tile([P, 2, N_H * D_H], U8, align_bytes=64)
-        for which in range(2):
-            quantise_weight(
-                nc, consts, "w2%d" % which, w2_raw[:, which], w2_codes[:, which, :], w2_scales[:, which, :]
+            regroup(nc.vector.tensor_copy, wc_grouped[:, g], wc_raw[:, g])
+        nc.vector.quantize_mx(
+            out=wc_codes[:].rearrange("p g c -> p (g c)").bitcast(FP8X4),
+            scales=wc_scales[:].rearrange("p g c -> p (g c)"),
+            in_=wc_grouped[:].rearrange("p g c t -> p (g c t)"),
+        )
+        w2_grouped = consts.tile([P, 2, D_OUT, PACK], BF16, align_bytes=64)
+        w2_codes = consts.tile([P, 2, D_OUT], U32, align_bytes=64)
+        w2_scales = consts.tile([P, 2, D_OUT], U8, align_bytes=64)
+
+        def quantise_second_weights():
+            regroup(nc.vector.tensor_copy, w2_grouped[:, 0], w2_raw[:, 0])
+            regroup(nc.scalar.copy, w2_grouped[:, 1], w2_raw[:, 1])
+            nc.vector.quantize_mx(
+                out=w2_codes[:].rearrange("p w c -> p (w c)").bitcast(FP8X4),
+                scales=w2_scales[:].rearrange("p w c -> p (w c)"),
+                in_=w2_grouped[:].rearrange("p w c t -> p (w c t)"),
             )
 
         steps = [(b, first) for b in range(B) for first in range(0, TILES, STEP)]
+        h_grouped = {}
         h_mx = {}
+        c_grouped = {}
         c_mx = {}
         out_tiles = {}
 
-        def transpose_and_quantise_h(n):
+        def transpose_h(n):
             b, first = steps[n]
             x_words = x_tiles[(b, first // HALF)][:].rearrange("p t k -> p (t k)").bitcast(F32)
-            grouped = work.tile([P, STEP * PASSES_1 * P * PACK], BF16, name="h_grouped", align_bytes=64)
-            grouped_words = grouped[:].bitcast(F32).rearrange(
+            h_grouped[n] = work.tile([P, STEP * PASSES_1 * P * PACK], BF16, name="h_grouped", align_bytes=64)
+            grouped_words = h_grouped[n][:].bitcast(F32).rearrange(
                 "p (i g r u) -> p i g r u", i=STEP, g=PASSES_1, u=2
             )
+            banks = []
             for i in range(STEP):
                 word0 = ((first + i) % HALF) * (D_MODEL // 2)
                 xt = psum.tile([P, 2 * PASSES_1, P], F32, name="xt")
                 for a in range(2 * PASSES_1):
                     nc.tensor.transpose(xt[:, a, :], x_words[:, word0 + a * P : word0 + (a + 1) * P], identity[:])
-                nc.scalar.copy(out=grouped_words[:, i], in_=xt[:].rearrange("p (g u) r -> p g r u", u=2))
+                banks.append(xt)
+            for i in range(STEP):
+                nc.scalar.copy(out=grouped_words[:, i], in_=banks[i][:].rearrange("p (g u) r -> p g r u", u=2))
+
+        def quantise_h(n):
             codes = work.tile([P, STEP, PASSES_1, P], U32, name="h_codes", align_bytes=64)
             scales = work.tile([P, STEP, PASSES_1, P], U8, name="h_scales", align_bytes=64)
             nc.vector.quantize_mx(
                 out=codes[:].rearrange("p i g r -> p (i g r)").bitcast(FP8X4),
                 scales=scales[:].rearrange("p i g r -> p (i g r)"),
-                in_=grouped[:],
+                in_=h_grouped[n][:],
             )
             h_mx[n] = (codes, scales)
 
-        def compress_and_quantise(n):
+        def compress(n):
             codes_h, scales_h = h_mx[n]
-            grouped = work.tile([P, STEP, P, PACK], BF16, name="c_grouped", align_bytes=64)
+            c_grouped[n] = work.tile([P, STEP, P, PACK], BF16, name="c_grouped", align_bytes=64)
+            banks = []
             for i in range(STEP):
                 cq = psum.tile([P, PACK, P], F32, name="cq")
                 for t in range(PACK):
@@ -180,28 +197,38 @@ def tile_mla_pa_t_kernel(tc, h, w_cq, w_q, w_qr, out):
                             start=(g == 0),
                             stop=(g == PASSES_1 - 1),
                         )
-                nc.scalar.copy(out=grouped[:, i], in_=cq[:].rearrange("p t r -> p r t"))
+                banks.append(cq)
+            for i in range(STEP):
+                nc.scalar.copy(out=c_grouped[n][:, i], in_=banks[i][:].rearrange("p t r -> p r t"))
+
+        def quantise_c(n):
             codes = work.tile([P, STEP, P], U32, name="c_codes", align_bytes=64)
             scales = work.tile([P, STEP, P], U8, name="c_scales", align_bytes=64)
             nc.vector.quantize_mx(
                 out=codes[:].rearrange("p i r -> p (i r)").bitcast(FP8X4),
                 scales=scales[:].rearrange("p i r -> p (i r)"),
-                in_=grouped[:].rearrange("p i r t -> p (i r t)"),
+                in_=c_grouped[n][:].rearrange("p i r t -> p (i r t)"),
             )
             c_mx[n] = (codes, scales)
+
+        def store(b, first, count):
+            rows = out[b].rearrange("n (p t) f -> p n t f", t=TILES)
+            q_tile = out_tiles[(b, first // HALF)]
+            nc.sync.dma_start(
+                out=rows[:, :, first : first + count, :],
+                in_=q_tile[:, :, first % HALF : first % HALF + count, :],
+            )
 
         def project_rotate_store(n):
             b, first = steps[n]
             codes_c, scales_c = c_mx[n]
-            half = first // HALF
             if first % HALF == 0:
-                out_tiles[(b, half)] = out_pool.tile([P, N_H, HALF, 2 * D_H], F32, name="q_tile")
-            q_tile = out_tiles[(b, half)]
+                out_tiles[(b, first // HALF)] = out_pool.tile([P, N_H, HALF, 2 * D_H], F32, name="q_tile")
+            q_tile = out_tiles[(b, first // HALF)]
+            banks = []
             for i in range(STEP):
-                t = first + i
-                products = []
                 for which, name in enumerate(("a_ps", "u_ps")):
-                    product = psum.tile([P, N_H * D_H], F32, name=name)
+                    product = psum.tile([P, D_OUT], F32, name=name)
                     nc.tensor.matmul_mx(
                         out=product[:],
                         lhsT=codes_c[:, i, :].bitcast(FP8X4),
@@ -211,39 +238,47 @@ def tile_mla_pa_t_kernel(tc, h, w_cq, w_q, w_qr, out):
                         start=True,
                         stop=True,
                     )
-                    products.append(product)
-                a_ps, u_ps = products
+                    banks.append(product)
+            for i in range(STEP):
+                t = first + i
+                a_ps, u_ps = banks[2 * i], banks[2 * i + 1]
                 nc.scalar.copy(
                     out=q_tile[:, :, t % HALF, 0:D_H], in_=a_ps[:].rearrange("p (n f) -> p n f", n=N_H)
                 )
-                rotated = q_tile[:, :, t % HALF, D_H : 2 * D_H]
-                nc.vector.tensor_tensor(
-                    out=rotated,
-                    in0=u_ps[:].rearrange("p (n f) -> p n f", n=N_H),
-                    in1=cos2[:, t].rearrange("p i e -> p (i e)").unsqueeze(1).to_broadcast([P, N_H, D_H]),
-                    op=MULT,
-                )
-                u_pairs = u_ps[:].rearrange("p (n i e) -> p n i e", n=N_H, e=2)
-                crossed = work.tile([P, 2, N_H, PAIRS], F32, name="crossed")
+                products = work.tile([P, 2, N_H, PAIRS, 2], F32, name="products")
                 for e in range(2):
+                    factors = table[:, t, 1 - e : 3 - e, :].rearrange("p x i -> p i x")
                     nc.vector.tensor_tensor(
-                        out=crossed[:, e],
-                        in0=u_pairs[:, :, :, 1 - e],
-                        in1=sin2[:, t, e, :].unsqueeze(1).to_broadcast([P, N_H, PAIRS]),
+                        out=products[:, e],
+                        in0=u_ps[:].rearrange("p (n i x) -> p n i x", n=N_H, x=2),
+                        in1=factors.unsqueeze(1).to_broadcast([P, N_H, PAIRS, 2]),
                         op=MULT,
                     )
-                rotated_pairs = rotated.rearrange("p n (i e) -> p n i e", e=2)
                 nc.gpsimd.tensor_tensor(
-                    out=rotated_pairs, in0=rotated_pairs, in1=crossed[:].rearrange("p e n i -> p n i e"), op=ADD
+                    out=q_tile[:, :, t % HALF, D_H : 2 * D_H].rearrange("p n (i e) -> p n i e", e=2),
+                    in0=products[:, :, :, :, 0].rearrange("p e n i -> p n i e"),
+                    in1=products[:, :, :, :, 1].rearrange("p e n i -> p n i e"),
+                    op=ADD,
                 )
-            if (first + STEP) % HALF == 0:
-                rows = out[b].rearrange("n (p t) f -> p n t f", t=TILES)
-                nc.sync.dma_start(out=rows[:, :, half * HALF : (half + 1) * HALF, :], in_=q_tile[:])
+            if n >= len(steps) - HALF // STEP:
+                store(b, first, STEP)
+            elif (first + STEP) % HALF == 0:
+                store(b, first + STEP - HALF, HALF)
 
-        for n in range(len(steps) + 2):
+        def step(n):
             if n < len(steps):
-                transpose_and_quantise_h(n)
+                transpose_h(n)
+            if n >= 2:
+                quantise_c(n - 2)
+            if n < len(steps):
+                quantise_h(n)
             if 1 <= n <= len(steps):
-                compress_and_quantise(n - 1)
+                compress(n - 1)
             if n >= 2:
                 project_rotate_store(n - 2)
+
+        step(0)
+        step(1)
+        quantise_second_weights()
+        for n in range(2, len(steps) + 2):
+            step(n)

@@ -152,6 +152,7 @@ def tile_mla_pa_t_kernel(tc, h, w_cq, w_q, w_qr, out):
         c_grouped = {}
         c_mx = {}
         out_tiles = {}
+        u_banks = {}
 
         def transpose_h(n):
             b, first = steps[n]
@@ -219,7 +220,7 @@ def tile_mla_pa_t_kernel(tc, h, w_cq, w_q, w_qr, out):
                 in_=q_tile[:, :, first % HALF : first % HALF + count, :],
             )
 
-        def project_rotate_store(n):
+        def project(n):
             b, first = steps[n]
             codes_c, scales_c = c_mx[n]
             if first % HALF == 0:
@@ -241,25 +242,33 @@ def tile_mla_pa_t_kernel(tc, h, w_cq, w_q, w_qr, out):
                     banks.append(product)
             for i in range(STEP):
                 t = first + i
-                a_ps, u_ps = banks[2 * i], banks[2 * i + 1]
                 nc.scalar.copy(
-                    out=q_tile[:, :, t % HALF, 0:D_H], in_=a_ps[:].rearrange("p (n f) -> p n f", n=N_H)
+                    out=q_tile[:, :, t % HALF, 0:D_H], in_=banks[2 * i][:].rearrange("p (n f) -> p n f", n=N_H)
                 )
-                products = work.tile([P, 2, N_H, PAIRS, 2], F32, name="products")
-                for e in range(2):
-                    factors = table[:, t, 1 - e : 3 - e, :].rearrange("p x i -> p i x")
-                    nc.vector.tensor_tensor(
-                        out=products[:, e],
-                        in0=u_ps[:].rearrange("p (n i x) -> p n i x", n=N_H, x=2),
-                        in1=factors.unsqueeze(1).to_broadcast([P, N_H, PAIRS, 2]),
-                        op=MULT,
-                    )
-                nc.gpsimd.tensor_tensor(
-                    out=q_tile[:, :, t % HALF, D_H : 2 * D_H].rearrange("p n (i e) -> p n i e", e=2),
-                    in0=products[:, :, :, :, 0].rearrange("p e n i -> p n i e"),
-                    in1=products[:, :, :, :, 1].rearrange("p e n i -> p n i e"),
-                    op=ADD,
+                u_banks[(n, i)] = banks[2 * i + 1]
+
+        def rotate(n, i):
+            b, first = steps[n]
+            t = first + i
+            q_tile = out_tiles[(b, first // HALF)]
+            products = work.tile([P, 2, N_H, PAIRS, 2], F32, name="products")
+            for e in range(2):
+                factors = table[:, t, 1 - e : 3 - e, :].rearrange("p x i -> p i x")
+                nc.vector.tensor_tensor(
+                    out=products[:, e],
+                    in0=u_banks[(n, i)][:].rearrange("p (n i x) -> p n i x", n=N_H, x=2),
+                    in1=factors.unsqueeze(1).to_broadcast([P, N_H, PAIRS, 2]),
+                    op=MULT,
                 )
+            nc.gpsimd.tensor_tensor(
+                out=q_tile[:, :, t % HALF, D_H : 2 * D_H].rearrange("p n (i e) -> p n i e", e=2),
+                in0=products[:, :, :, :, 0].rearrange("p e n i -> p n i e"),
+                in1=products[:, :, :, :, 1].rearrange("p e n i -> p n i e"),
+                op=ADD,
+            )
+
+        def store_step(n):
+            b, first = steps[n]
             if n >= len(steps) - HALF // STEP:
                 store(b, first, STEP)
             elif (first + STEP) % HALF == 0:
@@ -268,14 +277,17 @@ def tile_mla_pa_t_kernel(tc, h, w_cq, w_q, w_qr, out):
         def step(n):
             if n < len(steps):
                 transpose_h(n)
-            if n >= 2:
-                quantise_c(n - 2)
-            if n < len(steps):
                 quantise_h(n)
             if 1 <= n <= len(steps):
                 compress(n - 1)
             if n >= 2:
-                project_rotate_store(n - 2)
+                project(n - 2)
+                rotate(n - 2, 0)
+            if 1 <= n <= len(steps):
+                quantise_c(n - 1)
+            if n >= 2:
+                rotate(n - 2, 1)
+                store_step(n - 2)
 
         step(0)
         step(1)

@@ -24,6 +24,7 @@ TILES = S // P
 PAIRS = D_H // 2
 HALF = 4
 STEP = 2
+GPSIMD_HEADS = 3
 ROPE_BASE = 10000.0
 ROUND_MAGIC = 1.5 * 2.0**23
 
@@ -70,8 +71,8 @@ def rope_turn_fractions(nc, pool):
 
 def rope_table(nc, pool, sin_fraction, cos_fraction):
     table = pool.tile([P, TILES, 3, PAIRS], F32)
-    nc.scalar.activation(out=table[:, :, 0, :], in_=sin_fraction[:], func=SIN, scale=2.0 * math.pi)
-    nc.scalar.activation(out=table[:, :, 2, :], in_=sin_fraction[:], func=SIN, scale=-2.0 * math.pi)
+    nc.scalar.activation(out=table[:, :, 0, :], in_=sin_fraction[:], func=SIN, scale=-2.0 * math.pi)
+    nc.scalar.activation(out=table[:, :, 2, :], in_=sin_fraction[:], func=SIN, scale=2.0 * math.pi)
     nc.scalar.activation(out=table[:, :, 1, :], in_=cos_fraction[:], func=SIN, scale=2.0 * math.pi)
     return table
 
@@ -153,6 +154,7 @@ def tile_mla_pa_t_kernel(tc, h, w_cq, w_q, w_qr, out):
         c_mx = {}
         out_tiles = {}
         u_banks = {}
+        product_tiles = {}
 
         def transpose_h(n):
             b, first = steps[n]
@@ -249,48 +251,58 @@ def tile_mla_pa_t_kernel(tc, h, w_cq, w_q, w_qr, out):
 
         def rotate(n, i):
             b, first = steps[n]
-            t = first + i
             q_tile = out_tiles[(b, first // HALF)]
             products = work.tile([P, 2, N_H, PAIRS, 2], F32, name="products")
-            for e in range(2):
-                factors = table[:, t, 1 - e : 3 - e, :].rearrange("p x i -> p i x")
+            product_tiles[(n, i)] = products
+            u_pairs = u_banks[(n, i)][:].rearrange("p (n i x) -> p n i x", n=N_H, x=2)
+            for x in range(2):
+                factors = table[:, first + i, 1 - x : 3 - x, :].rearrange("p e i -> p i e")
                 nc.vector.tensor_tensor(
-                    out=products[:, e],
-                    in0=u_banks[(n, i)][:].rearrange("p (n i x) -> p n i x", n=N_H, x=2),
+                    out=products[:, x],
+                    in0=u_pairs[:, :, :, x].unsqueeze(3).to_broadcast([P, N_H, PAIRS, 2]),
                     in1=factors.unsqueeze(1).to_broadcast([P, N_H, PAIRS, 2]),
                     op=MULT,
                 )
             nc.gpsimd.tensor_tensor(
-                out=q_tile[:, :, t % HALF, D_H : 2 * D_H].rearrange("p n (i e) -> p n i e", e=2),
-                in0=products[:, :, :, :, 0].rearrange("p e n i -> p n i e"),
-                in1=products[:, :, :, :, 1].rearrange("p e n i -> p n i e"),
+                out=q_tile[:, 0:GPSIMD_HEADS, (first + i) % HALF, D_H : 2 * D_H],
+                in0=products[:, 0, 0:GPSIMD_HEADS].rearrange("p n i e -> p n (i e)"),
+                in1=products[:, 1, 0:GPSIMD_HEADS].rearrange("p n i e -> p n (i e)"),
                 op=ADD,
             )
 
-        def store_step(n):
+        def finish_rotation(n, i):
             b, first = steps[n]
+            q_tile = out_tiles[(b, first // HALF)]
+            nc.vector.tensor_reduce(
+                out=q_tile[:, GPSIMD_HEADS:N_H, (first + i) % HALF, D_H : 2 * D_H],
+                in_=product_tiles[(n, i)][:, :, GPSIMD_HEADS:N_H].rearrange("p x n i e -> p n (i e) x"),
+                axis=mybir.AxisListType.X,
+                op=ADD,
+            )
             if n >= len(steps) - HALF // STEP:
-                store(b, first, STEP)
-            elif (first + STEP) % HALF == 0:
-                store(b, first + STEP - HALF, HALF)
+                store(b, first + i, 1)
+            elif (first + i + 1) % HALF == 0:
+                store(b, first + i + 1 - HALF, HALF)
 
         def step(n):
             if n < len(steps):
                 transpose_h(n)
                 quantise_h(n)
+            if n >= 3:
+                finish_rotation(n - 3, 1)
             if 1 <= n <= len(steps):
                 compress(n - 1)
-            if n >= 2:
+            if 2 <= n <= len(steps) + 1:
                 project(n - 2)
                 rotate(n - 2, 0)
             if 1 <= n <= len(steps):
                 quantise_c(n - 1)
-            if n >= 2:
+            if 2 <= n <= len(steps) + 1:
+                finish_rotation(n - 2, 0)
                 rotate(n - 2, 1)
-                store_step(n - 2)
 
         step(0)
         step(1)
         quantise_second_weights()
-        for n in range(2, len(steps) + 2):
+        for n in range(2, len(steps) + 3):
             step(n)

@@ -24,7 +24,6 @@ TILES = S // P
 PAIRS = D_H // 2
 HALF = 4
 STEP = 2
-GPSIMD_HEADS = 3
 ROPE_BASE = 10000.0
 ROUND_MAGIC = 1.5 * 2.0**23
 
@@ -154,7 +153,6 @@ def tile_mla_pa_t_kernel(tc, h, w_cq, w_q, w_qr, out):
         c_mx = {}
         out_tiles = {}
         u_banks = {}
-        product_tiles = {}
 
         def transpose_h(n):
             b, first = steps[n]
@@ -253,7 +251,6 @@ def tile_mla_pa_t_kernel(tc, h, w_cq, w_q, w_qr, out):
             b, first = steps[n]
             q_tile = out_tiles[(b, first // HALF)]
             products = work.tile([P, 2, N_H, PAIRS, 2], F32, name="products")
-            product_tiles[(n, i)] = products
             u_pairs = u_banks[(n, i)][:].rearrange("p (n i x) -> p n i x", n=N_H, x=2)
             for x in range(2):
                 factors = table[:, first + i, 1 - x : 3 - x, :].rearrange("p e i -> p i e")
@@ -264,19 +261,9 @@ def tile_mla_pa_t_kernel(tc, h, w_cq, w_q, w_qr, out):
                     op=MULT,
                 )
             nc.gpsimd.tensor_tensor(
-                out=q_tile[:, 0:GPSIMD_HEADS, (first + i) % HALF, D_H : 2 * D_H],
-                in0=products[:, 0, 0:GPSIMD_HEADS].rearrange("p n i e -> p n (i e)"),
-                in1=products[:, 1, 0:GPSIMD_HEADS].rearrange("p n i e -> p n (i e)"),
-                op=ADD,
-            )
-
-        def finish_rotation(n, i):
-            b, first = steps[n]
-            q_tile = out_tiles[(b, first // HALF)]
-            nc.vector.tensor_reduce(
-                out=q_tile[:, GPSIMD_HEADS:N_H, (first + i) % HALF, D_H : 2 * D_H],
-                in_=product_tiles[(n, i)][:, :, GPSIMD_HEADS:N_H].rearrange("p x n i e -> p n (i e) x"),
-                axis=mybir.AxisListType.X,
+                out=q_tile[:, :, (first + i) % HALF, D_H : 2 * D_H],
+                in0=products[:, 0].rearrange("p n i e -> p n (i e)"),
+                in1=products[:, 1].rearrange("p n i e -> p n (i e)"),
                 op=ADD,
             )
             if n >= len(steps) - HALF // STEP:
@@ -284,25 +271,21 @@ def tile_mla_pa_t_kernel(tc, h, w_cq, w_q, w_qr, out):
             elif (first + i + 1) % HALF == 0:
                 store(b, first + i + 1 - HALF, HALF)
 
-        def step(n):
+        transpose_h(0)
+        quantise_h(0)
+        transpose_h(1)
+        quantise_h(1)
+        quantise_second_weights()
+        compress(0)
+        quantise_c(0)
+        for n in range(2, len(steps) + 2):
             if n < len(steps):
                 transpose_h(n)
                 quantise_h(n)
-            if n >= 3:
-                finish_rotation(n - 3, 1)
-            if 1 <= n <= len(steps):
+            if n <= len(steps):
                 compress(n - 1)
-            if 2 <= n <= len(steps) + 1:
-                project(n - 2)
-                rotate(n - 2, 0)
-            if 1 <= n <= len(steps):
+            project(n - 2)
+            rotate(n - 2, 0)
+            if n <= len(steps):
                 quantise_c(n - 1)
-            if 2 <= n <= len(steps) + 1:
-                finish_rotation(n - 2, 0)
-                rotate(n - 2, 1)
-
-        step(0)
-        step(1)
-        quantise_second_weights()
-        for n in range(2, len(steps) + 3):
-            step(n)
+            rotate(n - 2, 1)

@@ -24,6 +24,7 @@ TILES = S // P
 PAIRS = D_H // 2
 HALF = 4
 STEP = 2
+GPSIMD_HEADS = 3
 ROPE_BASE = 10000.0
 ROUND_MAGIC = 1.5 * 2.0**23
 
@@ -153,6 +154,7 @@ def tile_mla_pa_t_kernel(tc, h, w_cq, w_q, w_qr, out):
         c_mx = {}
         out_tiles = {}
         u_banks = {}
+        product_tiles = {}
 
         def transpose_h(n):
             b, first = steps[n]
@@ -247,10 +249,19 @@ def tile_mla_pa_t_kernel(tc, h, w_cq, w_q, w_qr, out):
                 )
                 u_banks[(n, i)] = banks[2 * i + 1]
 
+        def add_products(engine, n, i, heads):
+            b, first = steps[n]
+            engine.tensor_tensor(
+                out=out_tiles[(b, first // HALF)][:, heads, (first + i) % HALF, D_H : 2 * D_H],
+                in0=product_tiles[(n, i)][:, 0, heads].rearrange("p n i e -> p n (i e)"),
+                in1=product_tiles[(n, i)][:, 1, heads].rearrange("p n i e -> p n (i e)"),
+                op=ADD,
+            )
+
         def rotate(n, i):
             b, first = steps[n]
-            q_tile = out_tiles[(b, first // HALF)]
             products = work.tile([P, 2, N_H, PAIRS, 2], F32, name="products")
+            product_tiles[(n, i)] = products
             u_pairs = u_banks[(n, i)][:].rearrange("p (n i x) -> p n i x", n=N_H, x=2)
             for x in range(2):
                 factors = table[:, first + i, 1 - x : 3 - x, :].rearrange("p e i -> p i e")
@@ -260,12 +271,11 @@ def tile_mla_pa_t_kernel(tc, h, w_cq, w_q, w_qr, out):
                     in1=factors.unsqueeze(1).to_broadcast([P, N_H, PAIRS, 2]),
                     op=MULT,
                 )
-            nc.gpsimd.tensor_tensor(
-                out=q_tile[:, :, (first + i) % HALF, D_H : 2 * D_H],
-                in0=products[:, 0].rearrange("p n i e -> p n (i e)"),
-                in1=products[:, 1].rearrange("p n i e -> p n (i e)"),
-                op=ADD,
-            )
+            add_products(nc.gpsimd, n, i, slice(0, GPSIMD_HEADS))
+
+        def finish_rotation(n, i):
+            add_products(nc.vector, n, i, slice(GPSIMD_HEADS, N_H))
+            b, first = steps[n]
             if n >= len(steps) - HALF // STEP:
                 store(b, first + i, 1)
             elif (first + i + 1) % HALF == 0:
@@ -286,6 +296,10 @@ def tile_mla_pa_t_kernel(tc, h, w_cq, w_q, w_qr, out):
                 compress(n - 1)
             project(n - 2)
             rotate(n - 2, 0)
+            if n >= 3:
+                finish_rotation(n - 3, 1)
             if n <= len(steps):
                 quantise_c(n - 1)
             rotate(n - 2, 1)
+            finish_rotation(n - 2, 0)
+        finish_rotation(len(steps) - 1, 1)

import math
from contextlib import ExitStack

import concourse.mybir as mybir
from concourse.masks import make_identity

F32 = mybir.dt.float32
BF16 = mybir.dt.bfloat16
I32 = mybir.dt.int32
U32 = mybir.dt.uint32
U8 = mybir.dt.uint8
FP8X4 = mybir.dt.float8_e4m3fn_x4
MULT = mybir.AluOpType.mult
ADD = mybir.AluOpType.add
SUBTRACT = mybir.AluOpType.subtract
SIN = mybir.ActivationFunctionType.Sin

P = 128
PACK = 4
B, S, D_MODEL, N_H, D_H, D_CQ = 4, 1024, 1024, 4, 128, 512
D_OUT = N_H * D_H
PASSES_1 = D_MODEL // (P * PACK)
TILES = S // P
PAIRS = D_H // 2
HALF = 4
STEP = 2
GPSIMD_HEADS = 3
ROPE_BASE = 10000.0
ROUND_MAGIC = 1.5 * 2.0**23

FLOPS = 2 * B * S * (D_MODEL * D_CQ + D_CQ * 2 * D_OUT)


def rope_turn_fractions(nc, pool):
    position_i = pool.tile([P, TILES], I32)
    nc.gpsimd.iota(position_i[:], pattern=[[1, TILES]], base=0, channel_multiplier=TILES)
    position = pool.tile([P, TILES], F32)
    nc.vector.tensor_copy(out=position[:], in_=position_i[:])

    ratio = ROPE_BASE ** (-1.0 / PAIRS)
    freq = pool.tile([P, PAIRS], F32)
    nc.vector.memset(freq[:, 0:1], 1.0)
    for level in range(6):
        w = 2**level
        nc.vector.tensor_scalar_mul(out=freq[:, w : 2 * w], in0=freq[:, 0:w], scalar1=ratio**w)

    shape = [P, TILES, PAIRS]
    turns = pool.tile(shape, F32)
    nc.vector.scalar_tensor_tensor(
        out=turns[:],
        in0=freq[:].unsqueeze(1).to_broadcast(shape),
        scalar=1.0 / (2.0 * math.pi),
        in1=position[:].unsqueeze(2).to_broadcast(shape),
        op0=MULT,
        op1=MULT,
    )
    quarter = pool.tile(shape, F32)
    nc.vector.tensor_scalar_add(out=quarter[:], in0=turns[:], scalar1=0.25)

    fractions = []
    for name, angle in (("sin", turns), ("cos", quarter)):
        whole = pool.tile(shape, F32, name="whole_" + name)
        nc.vector.tensor_scalar(
            out=whole[:], in0=angle[:], scalar1=ROUND_MAGIC, scalar2=ROUND_MAGIC, op0=ADD, op1=SUBTRACT
        )
        fraction = pool.tile(shape, F32, name="fraction_" + name)
        nc.vector.tensor_sub(out=fraction[:], in0=angle[:], in1=whole[:])
        fractions.append(fraction)
    return fractions


def rope_table(nc, pool, sin_fraction, cos_fraction):
    table = pool.tile([P, TILES, 3, PAIRS], F32)
    nc.scalar.activation(out=table[:, :, 0, :], in_=sin_fraction[:], func=SIN, scale=-2.0 * math.pi)
    nc.scalar.activation(out=table[:, :, 2, :], in_=sin_fraction[:], func=SIN, scale=2.0 * math.pi)
    nc.scalar.activation(out=table[:, :, 1, :], in_=cos_fraction[:], func=SIN, scale=2.0 * math.pi)
    return table


def regroup(copy, grouped, raw):
    copy(
        out=grouped.rearrange("p (c i) t -> p c t i", i=4),
        in_=raw.rearrange("p t (c i) -> p c t i", i=4),
    )


def tile_mla_pa_t_kernel(tc, h, w_cq, w_q, w_qr, out):
    nc = tc.nc
    with ExitStack() as ctx:
        ctx.enter_context(tc.manual_schedule())
        consts = ctx.enter_context(tc.tile_pool(name="consts", bufs=1))
        x_pool = ctx.enter_context(tc.tile_pool(name="x", bufs=B * TILES // HALF))
        work = ctx.enter_context(tc.tile_pool(name="work", bufs=3))
        out_pool = ctx.enter_context(tc.tile_pool(name="outs", bufs=3))
        psum = ctx.enter_context(tc.psum_pool(name="psum", bufs=STEP))

        halves = [(b, half) for b in range(B) for half in range(TILES // HALF)]
        x_tiles = {}
        for b, half in halves:
            x_tiles[(b, half)] = x_pool.tile([P, HALF, D_MODEL], BF16, name="x")

        def load_h(b, half, first, count):
            rows = h[b].rearrange("(p t) k -> p t k", t=TILES)
            nc.sync.dma_start(
                out=x_tiles[(b, half)][:, first : first + count, :],
                in_=rows[:, half * HALF + first : half * HALF + first + count, :],
            )

        wc_raw = consts.tile([P, PASSES_1, PACK, D_CQ], BF16)
        w2_raw = consts.tile([P, 2, PACK, D_OUT], BF16)
        nc.sync.dma_start(
            out=wc_raw[:].rearrange("p g (u e) c -> p (g u) (e c)", u=2),
            in_=w_cq.rearrange("(a q e) c -> q a (e c)", a=2 * PASSES_1, e=2),
        )
        load_h(0, 0, 0, STEP)
        load_h(0, 0, STEP, STEP)
        nc.sync.dma_start(out=w2_raw[:, 0], in_=w_q.rearrange("(t p) n -> p t n", p=P))
        nc.sync.dma_start(out=w2_raw[:, 1], in_=w_qr.rearrange("(t p) n -> p t n", p=P))
        for b, half in halves[1:]:
            load_h(b, half, 0, HALF)

        sin_fraction, cos_fraction = rope_turn_fractions(nc, consts)
        table = rope_table(nc, consts, sin_fraction, cos_fraction)
        identity = consts.tile([P, P], F32)
        make_identity(nc, identity[:])

        wc_grouped = consts.tile([P, PASSES_1, D_CQ, PACK], BF16, align_bytes=64)
        wc_codes = consts.tile([P, PASSES_1, D_CQ], U32, align_bytes=64)
        wc_scales = consts.tile([P, PASSES_1, D_CQ], U8, align_bytes=64)
        for g in range(PASSES_1):
            regroup(nc.vector.tensor_copy, wc_grouped[:, g], wc_raw[:, g])
        nc.vector.quantize_mx(
            out=wc_codes[:].rearrange("p g c -> p (g c)").bitcast(FP8X4),
            scales=wc_scales[:].rearrange("p g c -> p (g c)"),
            in_=wc_grouped[:].rearrange("p g c t -> p (g c t)"),
        )
        w2_grouped = consts.tile([P, 2, D_OUT, PACK], BF16, align_bytes=64)
        w2_codes = consts.tile([P, 2, D_OUT], U32, align_bytes=64)
        w2_scales = consts.tile([P, 2, D_OUT], U8, align_bytes=64)

        def quantise_second_weights():
            regroup(nc.vector.tensor_copy, w2_grouped[:, 0], w2_raw[:, 0])
            regroup(nc.scalar.copy, w2_grouped[:, 1], w2_raw[:, 1])
            nc.vector.quantize_mx(
                out=w2_codes[:].rearrange("p w c -> p (w c)").bitcast(FP8X4),
                scales=w2_scales[:].rearrange("p w c -> p (w c)"),
                in_=w2_grouped[:].rearrange("p w c t -> p (w c t)"),
            )

        steps = [(b, first) for b in range(B) for first in range(0, TILES, STEP)]
        h_grouped = {}
        h_mx = {}
        c_grouped = {}
        c_mx = {}
        out_tiles = {}
        u_banks = {}
        product_tiles = {}

        def transpose_h(n):
            b, first = steps[n]
            x_words = x_tiles[(b, first // HALF)][:].rearrange("p t k -> p (t k)").bitcast(F32)
            h_grouped[n] = work.tile([P, STEP * PASSES_1 * P * PACK], BF16, name="h_grouped", align_bytes=64)
            grouped_words = h_grouped[n][:].bitcast(F32).rearrange(
                "p (i g r u) -> p i g r u", i=STEP, g=PASSES_1, u=2
            )
            banks = []
            for i in range(STEP):
                word0 = ((first + i) % HALF) * (D_MODEL // 2)
                xt = psum.tile([P, 2 * PASSES_1, P], F32, name="xt")
                for a in range(2 * PASSES_1):
                    nc.tensor.transpose(xt[:, a, :], x_words[:, word0 + a * P : word0 + (a + 1) * P], identity[:])
                banks.append(xt)
            for i in range(STEP):
                nc.scalar.copy(out=grouped_words[:, i], in_=banks[i][:].rearrange("p (g u) r -> p g r u", u=2))

        def quantise_h(n):
            codes = work.tile([P, STEP, PASSES_1, P], U32, name="h_codes", align_bytes=64)
            scales = work.tile([P, STEP, PASSES_1, P], U8, name="h_scales", align_bytes=64)
            nc.vector.quantize_mx(
                out=codes[:].rearrange("p i g r -> p (i g r)").bitcast(FP8X4),
                scales=scales[:].rearrange("p i g r -> p (i g r)"),
                in_=h_grouped[n][:],
            )
            h_mx[n] = (codes, scales)

        def compress(n):
            codes_h, scales_h = h_mx[n]
            c_grouped[n] = work.tile([P, STEP, P, PACK], BF16, name="c_grouped", align_bytes=64)
            banks = []
            for i in range(STEP):
                cq = psum.tile([P, PACK, P], F32, name="cq")
                for t in range(PACK):
                    for g in range(PASSES_1):
                        nc.tensor.matmul_mx(
                            out=cq[:, t, :],
                            lhsT=wc_codes[:, g, t * P : (t + 1) * P].bitcast(FP8X4),
                            lhsT_scale=wc_scales[:, g, t * P : (t + 1) * P],
                            rhs=codes_h[:, i, g, :].bitcast(FP8X4),
                            rhs_scale=scales_h[:, i, g, :],
                            start=(g == 0),
                            stop=(g == PASSES_1 - 1),
                        )
                banks.append(cq)
            for i in range(STEP):
                nc.scalar.copy(out=c_grouped[n][:, i], in_=banks[i][:].rearrange("p t r -> p r t"))

        def quantise_c(n):
            codes = work.tile([P, STEP, P], U32, name="c_codes", align_bytes=64)
            scales = work.tile([P, STEP, P], U8, name="c_scales", align_bytes=64)
            nc.vector.quantize_mx(
                out=codes[:].rearrange("p i r -> p (i r)").bitcast(FP8X4),
                scales=scales[:].rearrange("p i r -> p (i r)"),
                in_=c_grouped[n][:].rearrange("p i r t -> p (i r t)"),
            )
            c_mx[n] = (codes, scales)

        def store(b, first, count):
            rows = out[b].rearrange("n (p t) f -> p n t f", t=TILES)
            q_tile = out_tiles[(b, first // HALF)]
            nc.sync.dma_start(
                out=rows[:, :, first : first + count, :],
                in_=q_tile[:, :, first % HALF : first % HALF + count, :],
            )

        def project(n):
            b, first = steps[n]
            codes_c, scales_c = c_mx[n]
            if first % HALF == 0:
                out_tiles[(b, first // HALF)] = out_pool.tile([P, N_H, HALF, 2 * D_H], F32, name="q_tile")
            q_tile = out_tiles[(b, first // HALF)]
            banks = []
            for i in range(STEP):
                for which, name in enumerate(("a_ps", "u_ps")):
                    product = psum.tile([P, D_OUT], F32, name=name)
                    nc.tensor.matmul_mx(
                        out=product[:],
                        lhsT=codes_c[:, i, :].bitcast(FP8X4),
                        lhsT_scale=scales_c[:, i, :],
                        rhs=w2_codes[:, which, :].bitcast(FP8X4),
                        rhs_scale=w2_scales[:, which, :],
                        start=True,
                        stop=True,
                    )
                    banks.append(product)
            for i in range(STEP):
                t = first + i
                nc.scalar.copy(
                    out=q_tile[:, :, t % HALF, 0:D_H], in_=banks[2 * i][:].rearrange("p (n f) -> p n f", n=N_H)
                )
                u_banks[(n, i)] = banks[2 * i + 1]

        def add_products(engine, n, i, heads):
            b, first = steps[n]
            engine.tensor_tensor(
                out=out_tiles[(b, first // HALF)][:, heads, (first + i) % HALF, D_H : 2 * D_H],
                in0=product_tiles[(n, i)][:, 0, heads].rearrange("p n i e -> p n (i e)"),
                in1=product_tiles[(n, i)][:, 1, heads].rearrange("p n i e -> p n (i e)"),
                op=ADD,
            )

        def rotate(n, i):
            b, first = steps[n]
            products = work.tile([P, 2, N_H, PAIRS, 2], F32, name="products")
            product_tiles[(n, i)] = products
            u_pairs = u_banks[(n, i)][:].rearrange("p (n i x) -> p n i x", n=N_H, x=2)
            for x in range(2):
                factors = table[:, first + i, 1 - x : 3 - x, :].rearrange("p e i -> p i e")
                nc.vector.tensor_tensor(
                    out=products[:, x],
                    in0=u_pairs[:, :, :, x].unsqueeze(3).to_broadcast([P, N_H, PAIRS, 2]),
                    in1=factors.unsqueeze(1).to_broadcast([P, N_H, PAIRS, 2]),
                    op=MULT,
                )
            add_products(nc.gpsimd, n, i, slice(0, GPSIMD_HEADS))

        def finish_rotation(n, i):
            add_products(nc.vector, n, i, slice(GPSIMD_HEADS, N_H))
            b, first = steps[n]
            if n >= len(steps) - HALF // STEP:
                store(b, first + i, 1)
            elif (first + i + 1) % HALF == 0:
                store(b, first + i + 1 - HALF, HALF)

        transpose_h(0)
        quantise_h(0)
        transpose_h(1)
        quantise_h(1)
        quantise_second_weights()
        compress(0)
        quantise_c(0)
        for n in range(2, len(steps) + 2):
            if n < len(steps):
                transpose_h(n)
                quantise_h(n)
            if n <= len(steps):
                compress(n - 1)
            project(n - 2)
            rotate(n - 2, 0)
            if n >= 3:
                finish_rotation(n - 3, 1)
            if n <= len(steps):
                quantise_c(n - 1)
            rotate(n - 2, 1)
            finish_rotation(n - 2, 0)
        finish_rotation(len(steps) - 1, 1)
